import numpy as np
import ml_dtypes


def mxq(x, axis, fmt="e4m3"):
    dtype, down = {"e4m3": (ml_dtypes.float8_e4m3fn, 7), "e5m2": (ml_dtypes.float8_e5m2, 14)}[fmt]
    v = np.moveaxis(np.asarray(x, np.float32).astype(ml_dtypes.bfloat16).astype(np.float64), axis, -1)
    blocks = v.reshape(v.shape[:-1] + (-1, 32))
    amax = np.abs(blocks).max(-1, keepdims=True)
    byte = np.maximum(np.where(amax > 0, np.frexp(amax)[1] - 1 + 127, 0) - down, 1)
    scale = np.exp2(byte - 127.0)
    codes = (blocks / scale).astype(np.float32).astype(dtype).astype(np.float64)
    return np.moveaxis((codes * scale).reshape(v.shape), -1, axis)


WIDE = False


def mx_kscale(k):
    if not WIDE:
        return np.ones(k)
    levels = np.array([10, -10, 5, -5, 0])
    a = np.random.permutation(np.resize(levels, k // 512 * 4)).reshape(k // 512, 4)
    idx = np.arange(k)
    return np.exp2(a[idx // 512, idx % 128 // 32])


BF16 = ml_dtypes.bfloat16


def bf(x):
    return np.asarray(x, np.float32).astype(BF16)


def f64(x):
    return np.asarray(x).astype(np.float64)


E2M1 = np.array([0.0, 0.5, 1.0, 1.5, 2.0, 3.0, 4.0, 6.0, -0.0, -0.5, -1.0, -1.5, -2.0, -3.0, -4.0, -6.0])


def pack_weight(w, fmt):
    k, n = w.shape
    w = f64(bf(w)).reshape(k // 32, 32, n)
    amax = np.abs(w).max(1)
    if fmt == "e4m3":
        byte = np.frexp(amax)[1] - 1 + 127 - 7
    else:
        mant, ex = np.frexp(amax / 6.0)
        byte = np.where(mant > 0.5, ex, ex - 1) + 127
    byte = np.clip(np.where(amax > 0, byte, 1), 1, 254)
    scaled = (w * np.exp2(127.0 - byte)[:, None, :]).reshape(k, n).astype(np.float32)
    by_word = np.ascontiguousarray(scaled.reshape(k // 512, 128, 4, n).transpose(0, 1, 3, 2))
    if fmt == "e4m3":
        words = by_word.astype(ml_dtypes.float8_e4m3fn).view(np.uint8)
    else:
        c = by_word.astype(ml_dtypes.float4_e2m1fn).view(np.uint8) & 0xF
        words = c[..., 0::2] | (c[..., 1::2] << 4)
    return np.ascontiguousarray(words), np.ascontiguousarray(byte.astype(np.uint8).reshape(k // 512, 16, n))


def unpack_weight(words, scales, fmt):
    g, p, n, _ = words.shape
    if fmt == "e4m3":
        vals = np.ascontiguousarray(words).view(ml_dtypes.float8_e4m3fn).astype(np.float64)
    else:
        nib = np.empty((g, p, n, 4), np.uint8)
        nib[..., 0::2] = words & 0xF
        nib[..., 1::2] = words >> 4
        vals = E2M1[nib]
    vals = vals * np.repeat(np.exp2(scales.astype(np.float64) - 127.0), 8, axis=1)[..., None]
    return vals.transpose(0, 1, 3, 2).reshape(g * 512, n)


B, DIN, DOUT = 128, 1024, 2048
FMT = "e4m3"


def sigmoid(v):
    return 1.0 / (1.0 + np.exp(-v))


def setup_inputs():
    s, t = mx_kscale(DIN), mx_kscale(DOUT)
    inp = {"x": bf(np.random.standard_normal((B, DIN)) * s),
           "h": bf(np.random.standard_normal((B, DOUT)) * t),
           "c": bf(np.random.standard_normal((B, DOUT)))}
    for n in "ifgo":
        inp["Wx" + n + "_words"], inp["Wx" + n + "_scales"] = pack_weight(np.random.standard_normal((DIN, DOUT)) * 0.7 / np.sqrt(DIN) / s[:, None], FMT)
        inp["Wh" + n + "_words"], inp["Wh" + n + "_scales"] = pack_weight(np.random.standard_normal((DOUT, DOUT)) * 0.7 / np.sqrt(DOUT) / t[:, None], FMT)
        inp["bx" + n] = bf(np.random.standard_normal(DOUT) * 0.3)
        inp["bh" + n] = bf(np.random.standard_normal(DOUT) * 0.3)
    return inp


def reference(x, h, c,
              Wxi_words, Wxi_scales, Whi_words, Whi_scales, bxi, bhi,
              Wxf_words, Wxf_scales, Whf_words, Whf_scales, bxf, bhf,
              Wxg_words, Wxg_scales, Whg_words, Whg_scales, bxg, bhg,
              Wxo_words, Wxo_scales, Who_words, Who_scales, bxo, bho):
    Wx = np.concatenate([unpack_weight(Wxi_words, Wxi_scales, FMT), unpack_weight(Wxf_words, Wxf_scales, FMT), unpack_weight(Wxg_words, Wxg_scales, FMT), unpack_weight(Wxo_words, Wxo_scales, FMT)], axis=1)
    Wh = np.concatenate([unpack_weight(Whi_words, Whi_scales, FMT), unpack_weight(Whf_words, Whf_scales, FMT), unpack_weight(Whg_words, Whg_scales, FMT), unpack_weight(Who_words, Who_scales, FMT)], axis=1)
    b = np.concatenate([f64(bxi) + f64(bhi), f64(bxf) + f64(bhf), f64(bxg) + f64(bhg), f64(bxo) + f64(bho)])
    z = (mxq(f64(x), 1, "e4m3") @ Wx) + (mxq(f64(h), 1, "e4m3") @ Wh) + b
    zi, zf, zg, zo = np.split(z, 4, axis=1)
    i = sigmoid(zi)
    f = sigmoid(zf)
    g = np.tanh(zg)
    o = sigmoid(zo)
    c_new = f * f64(c) + i * g
    h_new = o * np.tanh(c_new)
    return (h_new, c_new)

@@ -1,0 +1,231 @@
+from contextlib import ExitStack
+
+import concourse.mybir as mybir
+from concourse.masks import make_identity
+
+F32 = mybir.dt.float32
+BF16 = mybir.dt.bfloat16
+I32 = mybir.dt.int32
+U32 = mybir.dt.uint32
+U8 = mybir.dt.uint8
+FP8X4 = mybir.dt.float8_e4m3fn_x4
+ACT = mybir.ActivationFunctionType
+ALU = mybir.AluOpType
+
+P = 128
+DIN = 1024
+DOUT = 2048
+NBLK = 512
+PASSES = 6
+NB = 12
+FLOPS = 2 * P * (DIN + DOUT) * 4 * DOUT
+
+
+def tile_lstmcell_w_kernel(tc, x, h, c, *rest):
+    nc = tc.nc
+    groups = [rest[6 * n : 6 * n + 6] for n in range(4)]
+    h_out = rest[24]
+    c_out = rest[25]
+    seq = [groups[0], groups[2], groups[1], groups[3]]
+
+    with ExitStack() as ctx:
+        keep = ctx.enter_context(tc.tile_pool(name="keep", bufs=1))
+        wpool = ctx.enter_context(tc.tile_pool(name="wpool", bufs=NB))
+        work = ctx.enter_context(tc.tile_pool(name="work", bufs=4))
+        psum = ctx.enter_context(tc.psum_pool(name="psum", bufs=1))
+        ctx.enter_context(tc.manual_schedule())
+
+        x_sb = keep.tile([P, DIN], BF16, name="x_sb")
+        h_sb = keep.tile([P, DOUT], BF16, name="h_sb")
+        c_sb = keep.tile([P, DOUT], BF16, name="c_sb")
+        nc.sync.dma_start(out=x_sb[:], in_=x[:, :])
+        nc.sync.dma_start(out=h_sb[:], in_=h[:, :])
+
+        brow = keep.tile([P, NBLK], BF16, name="brow")
+        nc.vector.memset(brow[:], 0.0)
+        planes = keep.tile([P, 6, DOUT], U8, name="planes", align_bytes=64)
+        for idx in (4, 0, 1, 5, 2, 3):
+            nc.vector.memset(planes[:, idx, :].bitcast(I32), 0)
+
+        ident = keep.tile([P, P], F32, name="ident")
+        make_identity(nc, ident[:])
+        for s in range(4):
+            for t in range(2):
+                r0 = 8 * s + 4 * t
+                nc.gpsimd.dma_start(
+                    out=brow[r0 : r0 + 4, :],
+                    in_=seq[s][4 + t].rearrange("(c n) -> c n", c=4),
+                )
+        for s in range(4):
+            kx = 8 * (s % 2)
+            for q in (0, 2, 1, 3):
+                nc.gpsimd.dma_start(
+                    out=planes[32 * q + kx : 32 * q + kx + 8, 4 + s // 2, :].bitcast(F32),
+                    in_=seq[s][1][:, 4 * q : 4 * q + 4, :].bitcast(F32),
+                )
+            for q in (0, 2, 1, 3):
+                nc.gpsimd.dma_start(
+                    out=planes[32 * q : 32 * q + 16, s, :].bitcast(F32),
+                    in_=seq[s][3][:, 4 * q : 4 * q + 4, :].bitcast(F32),
+                )
+
+        warm = keep.tile([P, 1], F32, name="warm")
+        nc.scalar.activation(out=warm[:], in_=ident[:, 0:1], func=ACT.Sigmoid)
+
+        sel = keep.tile([P, 16], BF16, name="sel")
+        idv = ident[:, 0:32].rearrange("p (s t c) -> p s t c", s=4, t=2)
+        nc.vector.tensor_tensor(
+            out=sel[:].rearrange("p (s c) -> p s c", s=4),
+            in0=idv[:, :, 0, :],
+            in1=idv[:, :, 1, :],
+            op=ALU.add,
+        )
+
+        units = []
+        for s in range(3):
+            for cp in range(PASSES):
+                units.append((s, cp, 0, 4))
+        for half in range(2):
+            for cp in range(PASSES):
+                units.append((3, cp, 2 * half, 2))
+        wtiles = {}
+
+        def load(u):
+            s, cp, j0, nj = units[u]
+            if (s, cp) not in wtiles:
+                wtiles[(s, cp)] = wpool.tile([P, DOUT], U32, name="w%d_%d" % (s, cp), tag="w", align_bytes=64)
+            wt = wtiles[(s, cp)]
+            src = seq[s][0][cp] if cp < 2 else seq[s][2][cp - 2]
+            src = src.rearrange("p n t -> p (n t)")
+            nc.sync.dma_start(
+                out=wt[:, NBLK * j0 : NBLK * (j0 + nj)].bitcast(I32),
+                in_=src[:, 4 * NBLK * j0 : 4 * NBLK * (j0 + nj)].bitcast(I32),
+            )
+
+        for u in range(NB):
+            load(u)
+        nc.sync.dma_start(out=c_sb[:], in_=c[:, :])
+
+        grouped = keep.tile([P, PASSES * 512], BF16, name="grouped", align_bytes=64)
+        a_codes = keep.tile([P, PASSES * P], U32, name="a_codes", align_bytes=64)
+        a_scl = keep.tile([P, PASSES * P], U8, name="a_scl", align_bytes=64)
+        xw = x_sb[:].bitcast(F32)
+        hw = h_sb[:].bitcast(F32)
+        srcs = [xw[:, 0:512], hw[:, 0:512], hw[:, 512:1024]]
+        for bk in range(3):
+            pt = psum.tile([P, 4, P], F32, name="pt%d" % bk, tag="bk%d" % (4 + bk))
+            for g in range(2):
+                for u in range(2):
+                    nc.tensor.transpose(pt[:, 2 * g + u, :], srcs[bk][:, 256 * g + u : 256 * (g + 1) : 2], ident[:])
+            nc.vector.tensor_copy(
+                out=grouped[:, 1024 * bk : 1024 * (bk + 1)].bitcast(F32).rearrange("p (g b u) -> p g b u", g=2, u=2),
+                in_=pt[:].rearrange("p (g u) b -> p g b u", g=2),
+            )
+            if bk == 1:
+                nc.vector.quantize_mx(
+                    out=a_codes[:, 0:256].bitcast(FP8X4), scales=a_scl[:, 0:256], in_=grouped[:, 0:1024]
+                )
+
+        bias = keep.tile([P, 4 * DOUT], F32, name="bias")
+
+        def bias_block(m):
+            pb = psum.tile([P, NBLK], F32, name="pb%d" % m, tag="bk%d" % (4 + (m + 3) % 4))
+            nc.tensor.matmul(out=pb[:], lhsT=sel[:, m : m + 1].to_broadcast([P, P]), rhs=brow[:], start=True, stop=True)
+            if m % 2 == 0:
+                nc.vector.tensor_copy(out=bias[:, NBLK * m : NBLK * (m + 1)], in_=pb[:])
+            else:
+                nc.scalar.copy(out=bias[:, NBLK * m : NBLK * (m + 1)], in_=pb[:])
+
+        bias_block(0)
+        nc.vector.quantize_mx(
+            out=a_codes[:, 256:768].bitcast(FP8X4), scales=a_scl[:, 256:768], in_=grouped[:, 1024:3072]
+        )
+        for m in range(1, 16):
+            bias_block(m)
+
+        ig = keep.tile([P, DOUT], F32, name="ig")
+        cn = keep.tile([P, DOUT], F32, name="cn")
+        tcn = keep.tile([P, DOUT], F32, name="tcn")
+        hn = keep.tile([P, DOUT], F32, name="hn")
+        banks = {}
+        zt = {}
+
+        def cols(j):
+            return slice(NBLK * j, NBLK * (j + 1))
+
+        def add_bias(s, j):
+            zt[j] = work.tile([P, NBLK], F32, name="z%d_%d" % (s, j), tag="z")
+            nc.vector.tensor_tensor(
+                out=zt[j][:], in0=banks[(s, j)][:], in1=bias[:, DOUT * s + NBLK * j : DOUT * s + NBLK * (j + 1)], op=ALU.add
+            )
+
+        def drain_i():
+            for j in range(4):
+                add_bias(0, j)
+                nc.scalar.activation(out=ig[:, cols(j)], in_=zt[j][:], func=ACT.Sigmoid)
+
+        def drain_g():
+            def fin(j):
+                nc.vector.tensor_tensor(out=ig[:, cols(j)], in0=ig[:, cols(j)], in1=zt[j][:], op=ALU.mult)
+
+            for j in range(4):
+                add_bias(1, j)
+                nc.scalar.activation(out=zt[j][:], in_=zt[j][:], func=ACT.Tanh)
+                if j >= 1:
+                    fin(j - 1)
+            fin(3)
+
+        def drain_f():
+            def fin(j):
+                nc.vector.tensor_tensor(out=zt[j][:], in0=zt[j][:], in1=c_sb[:, cols(j)], op=ALU.mult)
+                nc.vector.tensor_tensor(out=cn[:, cols(j)], in0=zt[j][:], in1=ig[:, cols(j)], op=ALU.add)
+                nc.scalar.activation(out=tcn[:, cols(j)], in_=cn[:, cols(j)], func=ACT.Tanh)
+
+            for j in range(4):
+                add_bias(2, j)
+                nc.scalar.activation(out=zt[j][:], in_=zt[j][:], func=ACT.Sigmoid)
+                if j >= 1:
+                    fin(j - 1)
+            fin(3)
+            nc.sync.dma_start(out=c_out[:, :], in_=cn[:])
+
+        def drain_o(j0):
+            for j in (j0, j0 + 1):
+                add_bias(3, j)
+                nc.scalar.activation(out=zt[j][:], in_=zt[j][:], func=ACT.Sigmoid)
+            for j in (j0, j0 + 1):
+                nc.vector.tensor_tensor(out=hn[:, cols(j)], in0=zt[j][:], in1=tcn[:, cols(j)], op=ALU.mult)
+            nc.sync.dma_start(out=h_out[:, NBLK * j0 : NBLK * (j0 + 2)], in_=hn[:, NBLK * j0 : NBLK * (j0 + 2)])
+
+        for u in range(len(units)):
+            s, cp, j0, nj = units[u]
+            if cp < 2:
+                idx = 4 + s // 2
+                k = 8 * (s % 2) + 4 * cp
+            else:
+                idx = s
+                k = 4 * (cp - 2)
+            wt = wtiles[(s, cp)]
+            for j in range(j0, j0 + nj):
+                if cp == 0:
+                    banks[(s, j)] = psum.tile([P, NBLK], F32, name="acc%d_%d" % (s, j), tag="bk%d" % (4 * (s % 2) + j))
+                nc.tensor.matmul_mx(
+                    out=banks[(s, j)][:],
+                    lhsT=a_codes[:, P * cp : P * (cp + 1)].bitcast(FP8X4),
+                    lhsT_scale=a_scl[:, P * cp : P * (cp + 1)],
+                    rhs=wt[:, cols(j)].bitcast(FP8X4),
+                    rhs_scale=planes[k:P, idx, cols(j)],
+                    start=(cp == 0),
+                    stop=(cp == PASSES - 1),
+                )
+            if u + NB < len(units):
+                load(u + NB)
+            if cp == PASSES - 1:
+                if s == 0:
+                    drain_i()
+                elif s == 1:
+                    drain_g()
+                elif s == 2:
+                    drain_f()
+                else:
+                    drain_o(j0)

@@ -56,18 +56,19 @@ def tile_lstmcell_w_kernel(tc, x, h, c, *rest):
                     out=brow[r0 : r0 + 4, :],
                     in_=seq[s][4 + t].rearrange("(c n) -> c n", c=4),
                 )
+        scale_dmas = []
         for s in range(4):
             kx = 8 * (s % 2)
             for q in (0, 2, 1, 3):
-                nc.gpsimd.dma_start(
-                    out=planes[32 * q + kx : 32 * q + kx + 8, 4 + s // 2, :].bitcast(F32),
-                    in_=seq[s][1][:, 4 * q : 4 * q + 4, :].bitcast(F32),
-                )
+                scale_dmas.append((planes[32 * q + kx : 32 * q + kx + 8, 4 + s // 2, :], seq[s][1][:, 4 * q : 4 * q + 4, :]))
             for q in (0, 2, 1, 3):
-                nc.gpsimd.dma_start(
-                    out=planes[32 * q : 32 * q + 16, s, :].bitcast(F32),
-                    in_=seq[s][3][:, 4 * q : 4 * q + 4, :].bitcast(F32),
-                )
+                scale_dmas.append((planes[32 * q : 32 * q + 16, s, :], seq[s][3][:, 4 * q : 4 * q + 4, :]))
+
+        def load_scales(first, last):
+            for dst, src in scale_dmas[first:last]:
+                nc.sync.dma_start(out=dst.bitcast(I32), in_=src.bitcast(I32))
+
+        load_scales(0, 4)
 
         warm = keep.tile([P, 1], F32, name="warm")
         nc.scalar.activation(out=warm[:], in_=ident[:, 0:1], func=ACT.Sigmoid)
@@ -104,6 +105,7 @@ def tile_lstmcell_w_kernel(tc, x, h, c, *rest):
 
         for u in range(NB):
             load(u)
+            load_scales(4 + 2 * u, 6 + 2 * u)
         nc.sync.dma_start(out=c_sb[:], in_=c[:, :])
 
         grouped = keep.tile([P, PASSES * 512], BF16, name="grouped", align_bytes=64)
@@ -220,6 +222,7 @@ def tile_lstmcell_w_kernel(tc, x, h, c, *rest):
                 )
             if u + NB < len(units):
                 load(u + NB)
+                load_scales(4 + 2 * (u + NB), 6 + 2 * (u + NB))
             if cp == PASSES - 1:
                 if s == 0:
                     drain_i()

@@ -20,6 +20,11 @@ PASSES = 6
 NB = 12
 FLOPS = 2 * P * (DIN + DOUT) * 4 * DOUT
 
+FULL_A = [[(0, 512, 0), (512, 512, 1), (1024, 512, 2), (1536, 512, 3)]]
+FULL_B = [[(0, 512, 4), (512, 512, 5), (1024, 512, 6), (1536, 512, 7)]]
+LAST = [[(0, 512, 4), (512, 512, 5), (1024, 256, 6)], [(1280, 512, 7)], [(1792, 256, 0)]]
+GROUPS = [FULL_A, FULL_B, FULL_A, LAST]
+
 
 def tile_lstmcell_w_kernel(tc, x, h, c, *rest):
     nc = tc.nc
@@ -49,26 +54,32 @@ def tile_lstmcell_w_kernel(tc, x, h, c, *rest):
 
         ident = keep.tile([P, P], F32, name="ident")
         make_identity(nc, ident[:])
-        for s in range(4):
-            for t in range(2):
-                r0 = 8 * s + 4 * t
-                nc.gpsimd.dma_start(
-                    out=brow[r0 : r0 + 4, :],
-                    in_=seq[s][4 + t].rearrange("(c n) -> c n", c=4),
-                )
-        scale_dmas = []
-        for s in range(4):
+
+        def load_bias_rows():
+            for s in range(4):
+                for t in range(2):
+                    r0 = 8 * s + 4 * t
+                    nc.gpsimd.dma_start(
+                        out=brow[r0 : r0 + 4, :],
+                        in_=seq[s][4 + t].rearrange("(c n) -> c n", c=4),
+                    )
+
+        def load_scale_rows(s):
             kx = 8 * (s % 2)
             for q in (0, 2, 1, 3):
-                scale_dmas.append((planes[32 * q + kx : 32 * q + kx + 8, 4 + s // 2, :], seq[s][1][:, 4 * q : 4 * q + 4, :]))
+                nc.gpsimd.dma_start(
+                    out=planes[32 * q + kx : 32 * q + kx + 8, 4 + s // 2, :].bitcast(F32),
+                    in_=seq[s][1][:, 4 * q : 4 * q + 4, :].bitcast(F32),
+                )
             for q in (0, 2, 1, 3):
-                scale_dmas.append((planes[32 * q : 32 * q + 16, s, :], seq[s][3][:, 4 * q : 4 * q + 4, :]))
+                nc.gpsimd.dma_start(
+                    out=planes[32 * q : 32 * q + 16, s, :].bitcast(F32),
+                    in_=seq[s][3][:, 4 * q : 4 * q + 4, :].bitcast(F32),
+                )
 
-        def load_scales(first, last):
-            for dst, src in scale_dmas[first:last]:
-                nc.sync.dma_start(out=dst.bitcast(I32), in_=src.bitcast(I32))
-
-        load_scales(0, 4)
+        load_bias_rows()
+        for s in range(4):
+            load_scale_rows(s)
 
         warm = keep.tile([P, 1], F32, name="warm")
         nc.scalar.activation(out=warm[:], in_=ident[:, 0:1], func=ACT.Sigmoid)
@@ -83,29 +94,26 @@ def tile_lstmcell_w_kernel(tc, x, h, c, *rest):
         )
 
         units = []
-        for s in range(3):
-            for cp in range(PASSES):
-                units.append((s, cp, 0, 4))
-        for half in range(2):
-            for cp in range(PASSES):
-                units.append((3, cp, 2 * half, 2))
+        for s in range(4):
+            for gi in range(len(GROUPS[s])):
+                for cp in range(PASSES):
+                    units.append((s, gi, cp))
         wtiles = {}
 
         def load(u):
-            s, cp, j0, nj = units[u]
+            s, gi, cp = units[u]
             if (s, cp) not in wtiles:
                 wtiles[(s, cp)] = wpool.tile([P, DOUT], U32, name="w%d_%d" % (s, cp), tag="w", align_bytes=64)
             wt = wtiles[(s, cp)]
+            blocks = GROUPS[s][gi]
+            lo = blocks[0][0]
+            hi = blocks[-1][0] + blocks[-1][1]
             src = seq[s][0][cp] if cp < 2 else seq[s][2][cp - 2]
             src = src.rearrange("p n t -> p (n t)")
-            nc.sync.dma_start(
-                out=wt[:, NBLK * j0 : NBLK * (j0 + nj)].bitcast(I32),
-                in_=src[:, 4 * NBLK * j0 : 4 * NBLK * (j0 + nj)].bitcast(I32),
-            )
+            nc.sync.dma_start(out=wt[:, lo:hi].bitcast(I32), in_=src[:, 4 * lo : 4 * hi].bitcast(I32))
 
         for u in range(NB):
             load(u)
-            load_scales(4 + 2 * u, 6 + 2 * u)
         nc.sync.dma_start(out=c_sb[:], in_=c[:, :])
 
         grouped = keep.tile([P, PASSES * 512], BF16, name="grouped", align_bytes=64)
@@ -152,55 +160,59 @@ def tile_lstmcell_w_kernel(tc, x, h, c, *rest):
         banks = {}
         zt = {}
 
-        def cols(j):
-            return slice(NBLK * j, NBLK * (j + 1))
+        def cols(blk):
+            return slice(blk[0], blk[0] + blk[1])
 
-        def add_bias(s, j):
-            zt[j] = work.tile([P, NBLK], F32, name="z%d_%d" % (s, j), tag="z")
+        def add_bias(s, blk):
+            zt[blk] = work.tile([P, blk[1]], F32, name="z%d_%d" % (s, blk[0]), tag="z")
             nc.vector.tensor_tensor(
-                out=zt[j][:], in0=banks[(s, j)][:], in1=bias[:, DOUT * s + NBLK * j : DOUT * s + NBLK * (j + 1)], op=ALU.add
+                out=zt[blk][:], in0=banks[(s, blk)][:], in1=bias[:, DOUT * s + blk[0] : DOUT * s + blk[0] + blk[1]], op=ALU.add
             )
 
-        def drain_i():
-            for j in range(4):
-                add_bias(0, j)
-                nc.scalar.activation(out=ig[:, cols(j)], in_=zt[j][:], func=ACT.Sigmoid)
+        def drain_i(blocks):
+            for blk in blocks:
+                add_bias(0, blk)
+                nc.scalar.activation(out=ig[:, cols(blk)], in_=zt[blk][:], func=ACT.Sigmoid)
 
-        def drain_g():
-            def fin(j):
-                nc.vector.tensor_tensor(out=ig[:, cols(j)], in0=ig[:, cols(j)], in1=zt[j][:], op=ALU.mult)
+        def drain_g(blocks):
+            def fin(blk):
+                nc.vector.tensor_tensor(out=ig[:, cols(blk)], in0=ig[:, cols(blk)], in1=zt[blk][:], op=ALU.mult)
 
-            for j in range(4):
-                add_bias(1, j)
-                nc.scalar.activation(out=zt[j][:], in_=zt[j][:], func=ACT.Tanh)
-                if j >= 1:
-                    fin(j - 1)
-            fin(3)
+            for n, blk in enumerate(blocks):
+                add_bias(1, blk)
+                nc.scalar.activation(out=zt[blk][:], in_=zt[blk][:], func=ACT.Tanh)
+                if n >= 1:
+                    fin(blocks[n - 1])
+            fin(blocks[-1])
 
-        def drain_f():
-            def fin(j):
-                nc.vector.tensor_tensor(out=zt[j][:], in0=zt[j][:], in1=c_sb[:, cols(j)], op=ALU.mult)
-                nc.vector.tensor_tensor(out=cn[:, cols(j)], in0=zt[j][:], in1=ig[:, cols(j)], op=ALU.add)
-                nc.scalar.activation(out=tcn[:, cols(j)], in_=cn[:, cols(j)], func=ACT.Tanh)
+        def drain_f(blocks):
+            def fin(blk):
+                nc.vector.tensor_tensor(out=zt[blk][:], in0=zt[blk][:], in1=c_sb[:, cols(blk)], op=ALU.mult)
+                nc.vector.tensor_tensor(out=cn[:, cols(blk)], in0=zt[blk][:], in1=ig[:, cols(blk)], op=ALU.add)
+                nc.scalar.activation(out=tcn[:, cols(blk)], in_=cn[:, cols(blk)], func=ACT.Tanh)
 
-            for j in range(4):
-                add_bias(2, j)
-                nc.scalar.activation(out=zt[j][:], in_=zt[j][:], func=ACT.Sigmoid)
-                if j >= 1:
-                    fin(j - 1)
-            fin(3)
+            for n, blk in enumerate(blocks):
+                add_bias(2, blk)
+                nc.scalar.activation(out=zt[blk][:], in_=zt[blk][:], func=ACT.Sigmoid)
+                if n >= 1:
+                    fin(blocks[n - 1])
+            fin(blocks[-1])
             nc.sync.dma_start(out=c_out[:, :], in_=cn[:])
 
-        def drain_o(j0):
-            for j in (j0, j0 + 1):
-                add_bias(3, j)
-                nc.scalar.activation(out=zt[j][:], in_=zt[j][:], func=ACT.Sigmoid)
-            for j in (j0, j0 + 1):
-                nc.vector.tensor_tensor(out=hn[:, cols(j)], in0=zt[j][:], in1=tcn[:, cols(j)], op=ALU.mult)
-            nc.sync.dma_start(out=h_out[:, NBLK * j0 : NBLK * (j0 + 2)], in_=hn[:, NBLK * j0 : NBLK * (j0 + 2)])
+        def drain_o(blocks):
+            for blk in blocks:
+                add_bias(3, blk)
+                nc.scalar.activation(out=zt[blk][:], in_=zt[blk][:], func=ACT.Sigmoid)
+            for blk in blocks:
+                nc.vector.tensor_tensor(out=hn[:, cols(blk)], in0=zt[blk][:], in1=tcn[:, cols(blk)], op=ALU.mult)
+            lo = blocks[0][0]
+            hi = blocks[-1][0] + blocks[-1][1]
+            nc.sync.dma_start(out=h_out[:, lo:hi], in_=hn[:, lo:hi])
 
+        drains = [drain_i, drain_g, drain_f, drain_o]
+        loaded = NB
         for u in range(len(units)):
-            s, cp, j0, nj = units[u]
+            s, gi, cp = units[u]
             if cp < 2:
                 idx = 4 + s // 2
                 k = 8 * (s % 2) + 4 * cp
@@ -208,27 +220,21 @@ def tile_lstmcell_w_kernel(tc, x, h, c, *rest):
                 idx = s
                 k = 4 * (cp - 2)
             wt = wtiles[(s, cp)]
-            for j in range(j0, j0 + nj):
+            for blk in GROUPS[s][gi]:
                 if cp == 0:
-                    banks[(s, j)] = psum.tile([P, NBLK], F32, name="acc%d_%d" % (s, j), tag="bk%d" % (4 * (s % 2) + j))
+                    banks[(s, blk)] = psum.tile([P, blk[1]], F32, name="acc%d_%d" % (s, blk[0]), tag="bk%d" % blk[2])
                 nc.tensor.matmul_mx(
-                    out=banks[(s, j)][:],
+                    out=banks[(s, blk)][:],
                     lhsT=a_codes[:, P * cp : P * (cp + 1)].bitcast(FP8X4),
                     lhsT_scale=a_scl[:, P * cp : P * (cp + 1)],
-                    rhs=wt[:, cols(j)].bitcast(FP8X4),
-                    rhs_scale=planes[k:P, idx, cols(j)],
+                    rhs=wt[:, cols(blk)].bitcast(FP8X4),
+                    rhs_scale=planes[k:P, idx, cols(blk)],
                     start=(cp == 0),
                     stop=(cp == PASSES - 1),
                 )
-            if u + NB < len(units):
-                load(u + NB)
-                load_scales(4 + 2 * (u + NB), 6 + 2 * (u + NB))
+            want = len(units) if u + NB >= 3 * PASSES + PASSES - 1 else u + NB + 1
+            while loaded < want:
+                load(loaded)
+                loaded += 1
             if cp == PASSES - 1:
-                if s == 0:
-                    drain_i()
-                elif s == 1:
-                    drain_g()
-                elif s == 2:
-                    drain_f()
-                else:
-                    drain_o(j0)
+                drains[s](GROUPS[s][gi])

@@ -55,14 +55,11 @@ def tile_lstmcell_w_kernel(tc, x, h, c, *rest):
         ident = keep.tile([P, P], F32, name="ident")
         make_identity(nc, ident[:])
 
-        def load_bias_rows():
-            for s in range(4):
-                for t in range(2):
-                    r0 = 8 * s + 4 * t
-                    nc.gpsimd.dma_start(
-                        out=brow[r0 : r0 + 4, :],
-                        in_=seq[s][4 + t].rearrange("(c n) -> c n", c=4),
-                    )
+        def load_bias_row(n):
+            nc.sync.dma_start(
+                out=brow[4 * n : 4 * n + 4, :],
+                in_=seq[n // 2][4 + n % 2].rearrange("(c n) -> c n", c=4),
+            )
 
         def load_scale_rows(s):
             kx = 8 * (s % 2)
@@ -77,7 +74,6 @@ def tile_lstmcell_w_kernel(tc, x, h, c, *rest):
                     in_=seq[s][3][:, 4 * q : 4 * q + 4, :].bitcast(F32),
                 )
 
-        load_bias_rows()
         for s in range(4):
             load_scale_rows(s)
 
@@ -114,6 +110,8 @@ def tile_lstmcell_w_kernel(tc, x, h, c, *rest):
 
         for u in range(NB):
             load(u)
+            if u < 8:
+                load_bias_row(u)
         nc.sync.dma_start(out=c_sb[:], in_=c[:, :])
 
         grouped = keep.tile([P, PASSES * 512], BF16, name="grouped", align_bytes=64)
@@ -146,12 +144,9 @@ def tile_lstmcell_w_kernel(tc, x, h, c, *rest):
             else:
                 nc.scalar.copy(out=bias[:, NBLK * m : NBLK * (m + 1)], in_=pb[:])
 
-        bias_block(0)
         nc.vector.quantize_mx(
             out=a_codes[:, 256:768].bitcast(FP8X4), scales=a_scl[:, 256:768], in_=grouped[:, 1024:3072]
         )
-        for m in range(1, 16):
-            bias_block(m)
 
         ig = keep.tile([P, DOUT], F32, name="ig")
         cn = keep.tile([P, DOUT], F32, name="cn")
@@ -236,5 +231,8 @@ def tile_lstmcell_w_kernel(tc, x, h, c, *rest):
             while loaded < want:
                 load(loaded)
                 loaded += 1
+            if u == 3:
+                for m in range(16):
+                    bias_block(m)
             if cp == PASSES - 1:
                 drains[s](GROUPS[s][gi])

@@ -25,6 +25,9 @@ FULL_B = [[(0, 512, 4), (512, 512, 5), (1024, 512, 6), (1536, 512, 7)]]
 LAST = [[(0, 512, 4), (512, 512, 5), (1024, 256, 6)], [(1280, 512, 7)], [(1792, 256, 0)]]
 GROUPS = [FULL_A, FULL_B, FULL_A, LAST]
 
+SINGLES = [[0], [1], [2], [3], [4], [5]]
+LOADS = [[SINGLES], [SINGLES], [SINGLES], [SINGLES, [[0, 1], [2, 3], [4, 5]], [[0, 1], [2, 3, 4], [5]]]]
+
 
 def tile_lstmcell_w_kernel(tc, x, h, c, *rest):
     nc = tc.nc
@@ -48,18 +51,21 @@ def tile_lstmcell_w_kernel(tc, x, h, c, *rest):
 
         brow = keep.tile([P, NBLK], BF16, name="brow")
         nc.vector.memset(brow[:], 0.0)
+
+        def load_bias_row(n):
+            nc.scalar.dma_start(
+                out=brow[4 * n : 4 * n + 4, :],
+                in_=seq[n // 2][4 + n % 2].rearrange("(c n) -> c n", c=4),
+            )
+
+        for n in range(4):
+            load_bias_row(n)
         planes = keep.tile([P, 6, DOUT], U8, name="planes", align_bytes=64)
         for idx in (4, 0, 1, 5, 2, 3):
             nc.vector.memset(planes[:, idx, :].bitcast(I32), 0)
 
         ident = keep.tile([P, P], F32, name="ident")
         make_identity(nc, ident[:])
-
-        def load_bias_row(n):
-            nc.sync.dma_start(
-                out=brow[4 * n : 4 * n + 4, :],
-                in_=seq[n // 2][4 + n % 2].rearrange("(c n) -> c n", c=4),
-            )
 
         def load_scale_rows(s):
             kx = 8 * (s % 2)
@@ -92,26 +98,33 @@ def tile_lstmcell_w_kernel(tc, x, h, c, *rest):
         units = []
         for s in range(4):
             for gi in range(len(GROUPS[s])):
-                for cp in range(PASSES):
-                    units.append((s, gi, cp))
+                for passes in LOADS[s][gi]:
+                    units.append((s, gi, passes))
         wtiles = {}
 
         def load(u):
-            s, gi, cp = units[u]
-            if (s, cp) not in wtiles:
-                wtiles[(s, cp)] = wpool.tile([P, DOUT], U32, name="w%d_%d" % (s, cp), tag="w", align_bytes=64)
-            wt = wtiles[(s, cp)]
+            s, gi, passes = units[u]
             blocks = GROUPS[s][gi]
             lo = blocks[0][0]
             hi = blocks[-1][0] + blocks[-1][1]
-            src = seq[s][0][cp] if cp < 2 else seq[s][2][cp - 2]
-            src = src.rearrange("p n t -> p (n t)")
-            nc.sync.dma_start(out=wt[:, lo:hi].bitcast(I32), in_=src[:, 4 * lo : 4 * hi].bitcast(I32))
+            shape = [P, len(passes), hi - lo]
+            if gi == 0:
+                wt = wpool.tile(shape, U32, name="w%d" % u, tag="w", align_bytes=64)
+            else:
+                wt = keep.tile(shape, U32, name="w%d" % u, align_bytes=64)
+            wtiles[u] = wt
+            if passes[0] < 2:
+                src = seq[s][0][passes[0] : passes[-1] + 1]
+            else:
+                src = seq[s][2][passes[0] - 2 : passes[-1] - 1]
+            src = src.rearrange("g p n t -> p g (n t)")
+            nc.sync.dma_start(out=wt[:].bitcast(I32), in_=src[:, :, 4 * lo : 4 * hi].bitcast(I32))
 
         for u in range(NB):
             load(u)
-            if u < 8:
-                load_bias_row(u)
+            if u == 1:
+                for n in range(4, 8):
+                    load_bias_row(n)
         nc.sync.dma_start(out=c_sb[:], in_=c[:, :])
 
         grouped = keep.tile([P, PASSES * 512], BF16, name="grouped", align_bytes=64)
@@ -207,26 +220,28 @@ def tile_lstmcell_w_kernel(tc, x, h, c, *rest):
         drains = [drain_i, drain_g, drain_f, drain_o]
         loaded = NB
         for u in range(len(units)):
-            s, gi, cp = units[u]
-            if cp < 2:
-                idx = 4 + s // 2
-                k = 8 * (s % 2) + 4 * cp
-            else:
-                idx = s
-                k = 4 * (cp - 2)
-            wt = wtiles[(s, cp)]
-            for blk in GROUPS[s][gi]:
-                if cp == 0:
-                    banks[(s, blk)] = psum.tile([P, blk[1]], F32, name="acc%d_%d" % (s, blk[0]), tag="bk%d" % blk[2])
-                nc.tensor.matmul_mx(
-                    out=banks[(s, blk)][:],
-                    lhsT=a_codes[:, P * cp : P * (cp + 1)].bitcast(FP8X4),
-                    lhsT_scale=a_scl[:, P * cp : P * (cp + 1)],
-                    rhs=wt[:, cols(blk)].bitcast(FP8X4),
-                    rhs_scale=planes[k:P, idx, cols(blk)],
-                    start=(cp == 0),
-                    stop=(cp == PASSES - 1),
-                )
+            s, gi, passes = units[u]
+            wt = wtiles[u]
+            lo = GROUPS[s][gi][0][0]
+            for j, cp in enumerate(passes):
+                if cp < 2:
+                    idx = 4 + s // 2
+                    k = 8 * (s % 2) + 4 * cp
+                else:
+                    idx = s
+                    k = 4 * (cp - 2)
+                for blk in GROUPS[s][gi]:
+                    if cp == 0:
+                        banks[(s, blk)] = psum.tile([P, blk[1]], F32, name="acc%d_%d" % (s, blk[0]), tag="bk%d" % blk[2])
+                    nc.tensor.matmul_mx(
+                        out=banks[(s, blk)][:],
+                        lhsT=a_codes[:, P * cp : P * (cp + 1)].bitcast(FP8X4),
+                        lhsT_scale=a_scl[:, P * cp : P * (cp + 1)],
+                        rhs=wt[:, j, blk[0] - lo : blk[0] - lo + blk[1]].bitcast(FP8X4),
+                        rhs_scale=planes[k:P, idx, cols(blk)],
+                        start=(cp == 0),
+                        stop=(cp == PASSES - 1),
+                    )
             want = len(units) if u + NB >= 3 * PASSES + PASSES - 1 else u + NB + 1
             while loaded < want:
                 load(loaded)
@@ -234,5 +249,5 @@ def tile_lstmcell_w_kernel(tc, x, h, c, *rest):
             if u == 3:
                 for m in range(16):
                     bias_block(m)
-            if cp == PASSES - 1:
+            if passes[-1] == PASSES - 1:
                 drains[s](GROUPS[s][gi])

@@ -49,6 +49,8 @@ def tile_lstmcell_w_kernel(tc, x, h, c, *rest):
         nc.sync.dma_start(out=x_sb[:], in_=x[:, :])
         nc.sync.dma_start(out=h_sb[:], in_=h[:, :])
 
+        planes = keep.tile([P, 6, DOUT], U8, name="planes", align_bytes=64)
+        nc.vector.memset(planes[:, 4, :].bitcast(I32), 0)
         brow = keep.tile([P, NBLK], BF16, name="brow")
         nc.vector.memset(brow[:], 0.0)
 
@@ -60,12 +62,8 @@ def tile_lstmcell_w_kernel(tc, x, h, c, *rest):
 
         for n in range(4):
             load_bias_row(n)
-        planes = keep.tile([P, 6, DOUT], U8, name="planes", align_bytes=64)
-        for idx in (4, 0, 1, 5, 2, 3):
+        for idx in (0, 1, 5, 2, 3):
             nc.vector.memset(planes[:, idx, :].bitcast(I32), 0)
-
-        ident = keep.tile([P, P], F32, name="ident")
-        make_identity(nc, ident[:])
 
         def load_scale_rows(s):
             kx = 8 * (s % 2)
@@ -74,17 +72,21 @@ def tile_lstmcell_w_kernel(tc, x, h, c, *rest):
                     out=planes[32 * q + kx : 32 * q + kx + 8, 4 + s // 2, :].bitcast(F32),
                     in_=seq[s][1][:, 4 * q : 4 * q + 4, :].bitcast(F32),
                 )
+            if s == 0:
+                make_identity(nc, ident[:])
             for q in (0, 2, 1, 3):
-                nc.gpsimd.dma_start(
-                    out=planes[32 * q : 32 * q + 16, s, :].bitcast(F32),
-                    in_=seq[s][3][:, 4 * q : 4 * q + 4, :].bitcast(F32),
+                nc.sync.dma_start(
+                    out=planes[32 * q : 32 * q + 16, s, :].bitcast(I32),
+                    in_=seq[s][3][:, 4 * q : 4 * q + 4, :].bitcast(I32),
                 )
 
+        ident = keep.tile([P, P], F32, name="ident")
         for s in range(4):
             load_scale_rows(s)
 
         warm = keep.tile([P, 1], F32, name="warm")
-        nc.scalar.activation(out=warm[:], in_=ident[:, 0:1], func=ACT.Sigmoid)
+        nc.vector.memset(warm[:], 0.0)
+        nc.scalar.activation(out=warm[:], in_=warm[:], func=ACT.Sigmoid)
 
         sel = keep.tile([P, 16], BF16, name="sel")
         idv = ident[:, 0:32].rearrange("p (s t c) -> p s t c", s=4, t=2)

from contextlib import ExitStack

import concourse.mybir as mybir
from concourse.masks import make_identity

F32 = mybir.dt.float32
BF16 = mybir.dt.bfloat16
I32 = mybir.dt.int32
U32 = mybir.dt.uint32
U8 = mybir.dt.uint8
FP8X4 = mybir.dt.float8_e4m3fn_x4
ACT = mybir.ActivationFunctionType
ALU = mybir.AluOpType

P = 128
DIN = 1024
DOUT = 2048
NBLK = 512
PASSES = 6
NB = 12
FLOPS = 2 * P * (DIN + DOUT) * 4 * DOUT

FULL_A = [[(0, 512, 0), (512, 512, 1), (1024, 512, 2), (1536, 512, 3)]]
FULL_B = [[(0, 512, 4), (512, 512, 5), (1024, 512, 6), (1536, 512, 7)]]
LAST = [[(0, 512, 4), (512, 512, 5), (1024, 256, 6)], [(1280, 512, 7)], [(1792, 256, 0)]]
GROUPS = [FULL_A, FULL_B, FULL_A, LAST]

SINGLES = [[0], [1], [2], [3], [4], [5]]
LOADS = [[SINGLES], [SINGLES], [SINGLES], [SINGLES, [[0, 1], [2, 3], [4, 5]], [[0, 1], [2, 3, 4], [5]]]]


def tile_lstmcell_w_kernel(tc, x, h, c, *rest):
    nc = tc.nc
    groups = [rest[6 * n : 6 * n + 6] for n in range(4)]
    h_out = rest[24]
    c_out = rest[25]
    seq = [groups[0], groups[2], groups[1], groups[3]]

    with ExitStack() as ctx:
        keep = ctx.enter_context(tc.tile_pool(name="keep", bufs=1))
        wpool = ctx.enter_context(tc.tile_pool(name="wpool", bufs=NB))
        work = ctx.enter_context(tc.tile_pool(name="work", bufs=4))
        psum = ctx.enter_context(tc.psum_pool(name="psum", bufs=1))
        ctx.enter_context(tc.manual_schedule())

        x_sb = keep.tile([P, DIN], BF16, name="x_sb")
        h_sb = keep.tile([P, DOUT], BF16, name="h_sb")
        c_sb = keep.tile([P, DOUT], BF16, name="c_sb")
        nc.sync.dma_start(out=x_sb[:], in_=x[:, :])
        nc.sync.dma_start(out=h_sb[:], in_=h[:, :])

        planes = keep.tile([P, 6, DOUT], U8, name="planes", align_bytes=64)
        nc.vector.memset(planes[:, 4, :].bitcast(I32), 0)
        brow = keep.tile([P, NBLK], BF16, name="brow")
        nc.vector.memset(brow[:], 0.0)

        def load_bias_row(n):
            nc.scalar.dma_start(
                out=brow[4 * n : 4 * n + 4, :],
                in_=seq[n // 2][4 + n % 2].rearrange("(c n) -> c n", c=4),
            )

        for n in range(4):
            load_bias_row(n)
        for idx in (0, 1, 5, 2, 3):
            nc.vector.memset(planes[:, idx, :].bitcast(I32), 0)

        def load_scale_rows(s):
            kx = 8 * (s % 2)
            for q in (0, 2, 1, 3):
                nc.gpsimd.dma_start(
                    out=planes[32 * q + kx : 32 * q + kx + 8, 4 + s // 2, :].bitcast(F32),
                    in_=seq[s][1][:, 4 * q : 4 * q + 4, :].bitcast(F32),
                )
            if s == 0:
                make_identity(nc, ident[:])
            for q in (0, 2, 1, 3):
                nc.sync.dma_start(
                    out=planes[32 * q : 32 * q + 16, s, :].bitcast(I32),
                    in_=seq[s][3][:, 4 * q : 4 * q + 4, :].bitcast(I32),
                )

        ident = keep.tile([P, P], F32, name="ident")
        for s in range(4):
            load_scale_rows(s)

        warm = keep.tile([P, 1], F32, name="warm")
        nc.vector.memset(warm[:], 0.0)
        nc.scalar.activation(out=warm[:], in_=warm[:], func=ACT.Sigmoid)

        sel = keep.tile([P, 16], BF16, name="sel")
        idv = ident[:, 0:32].rearrange("p (s t c) -> p s t c", s=4, t=2)
        nc.vector.tensor_tensor(
            out=sel[:].rearrange("p (s c) -> p s c", s=4),
            in0=idv[:, :, 0, :],
            in1=idv[:, :, 1, :],
            op=ALU.add,
        )

        units = []
        for s in range(4):
            for gi in range(len(GROUPS[s])):
                for passes in LOADS[s][gi]:
                    units.append((s, gi, passes))
        wtiles = {}

        def load(u):
            s, gi, passes = units[u]
            blocks = GROUPS[s][gi]
            lo = blocks[0][0]
            hi = blocks[-1][0] + blocks[-1][1]
            shape = [P, len(passes), hi - lo]
            if gi == 0:
                wt = wpool.tile(shape, U32, name="w%d" % u, tag="w", align_bytes=64)
            else:
                wt = keep.tile(shape, U32, name="w%d" % u, align_bytes=64)
            wtiles[u] = wt
            if passes[0] < 2:
                src = seq[s][0][passes[0] : passes[-1] + 1]
            else:
                src = seq[s][2][passes[0] - 2 : passes[-1] - 1]
            src = src.rearrange("g p n t -> p g (n t)")
            nc.sync.dma_start(out=wt[:].bitcast(I32), in_=src[:, :, 4 * lo : 4 * hi].bitcast(I32))

        for u in range(NB):
            load(u)
            if u == 1:
                for n in range(4, 8):
                    load_bias_row(n)
        nc.sync.dma_start(out=c_sb[:], in_=c[:, :])

        grouped = keep.tile([P, PASSES * 512], BF16, name="grouped", align_bytes=64)
        a_codes = keep.tile([P, PASSES * P], U32, name="a_codes", align_bytes=64)
        a_scl = keep.tile([P, PASSES * P], U8, name="a_scl", align_bytes=64)
        xw = x_sb[:].bitcast(F32)
        hw = h_sb[:].bitcast(F32)
        srcs = [xw[:, 0:512], hw[:, 0:512], hw[:, 512:1024]]
        for bk in range(3):
            pt = psum.tile([P, 4, P], F32, name="pt%d" % bk, tag="bk%d" % (4 + bk))
            for g in range(2):
                for u in range(2):
                    nc.tensor.transpose(pt[:, 2 * g + u, :], srcs[bk][:, 256 * g + u : 256 * (g + 1) : 2], ident[:])
            nc.vector.tensor_copy(
                out=grouped[:, 1024 * bk : 1024 * (bk + 1)].bitcast(F32).rearrange("p (g b u) -> p g b u", g=2, u=2),
                in_=pt[:].rearrange("p (g u) b -> p g b u", g=2),
            )
            if bk == 1:
                nc.vector.quantize_mx(
                    out=a_codes[:, 0:256].bitcast(FP8X4), scales=a_scl[:, 0:256], in_=grouped[:, 0:1024]
                )

        bias = keep.tile([P, 4 * DOUT], F32, name="bias")

        def bias_block(m):
            pb = psum.tile([P, NBLK], F32, name="pb%d" % m, tag="bk%d" % (4 + (m + 3) % 4))
            nc.tensor.matmul(out=pb[:], lhsT=sel[:, m : m + 1].to_broadcast([P, P]), rhs=brow[:], start=True, stop=True)
            if m % 2 == 0:
                nc.vector.tensor_copy(out=bias[:, NBLK * m : NBLK * (m + 1)], in_=pb[:])
            else:
                nc.scalar.copy(out=bias[:, NBLK * m : NBLK * (m + 1)], in_=pb[:])

        nc.vector.quantize_mx(
            out=a_codes[:, 256:768].bitcast(FP8X4), scales=a_scl[:, 256:768], in_=grouped[:, 1024:3072]
        )

        ig = keep.tile([P, DOUT], F32, name="ig")
        cn = keep.tile([P, DOUT], F32, name="cn")
        tcn = keep.tile([P, DOUT], F32, name="tcn")
        hn = keep.tile([P, DOUT], F32, name="hn")
        banks = {}
        zt = {}

        def cols(blk):
            return slice(blk[0], blk[0] + blk[1])

        def add_bias(s, blk):
            zt[blk] = work.tile([P, blk[1]], F32, name="z%d_%d" % (s, blk[0]), tag="z")
            nc.vector.tensor_tensor(
                out=zt[blk][:], in0=banks[(s, blk)][:], in1=bias[:, DOUT * s + blk[0] : DOUT * s + blk[0] + blk[1]], op=ALU.add
            )

        def drain_i(blocks):
            for blk in blocks:
                add_bias(0, blk)
                nc.scalar.activation(out=ig[:, cols(blk)], in_=zt[blk][:], func=ACT.Sigmoid)

        def drain_g(blocks):
            def fin(blk):
                nc.vector.tensor_tensor(out=ig[:, cols(blk)], in0=ig[:, cols(blk)], in1=zt[blk][:], op=ALU.mult)

            for n, blk in enumerate(blocks):
                add_bias(1, blk)
                nc.scalar.activation(out=zt[blk][:], in_=zt[blk][:], func=ACT.Tanh)
                if n >= 1:
                    fin(blocks[n - 1])
            fin(blocks[-1])

        def drain_f(blocks):
            def fin(blk):
                nc.vector.tensor_tensor(out=zt[blk][:], in0=zt[blk][:], in1=c_sb[:, cols(blk)], op=ALU.mult)
                nc.vector.tensor_tensor(out=cn[:, cols(blk)], in0=zt[blk][:], in1=ig[:, cols(blk)], op=ALU.add)
                nc.scalar.activation(out=tcn[:, cols(blk)], in_=cn[:, cols(blk)], func=ACT.Tanh)

            for n, blk in enumerate(blocks):
                add_bias(2, blk)
                nc.scalar.activation(out=zt[blk][:], in_=zt[blk][:], func=ACT.Sigmoid)
                if n >= 1:
                    fin(blocks[n - 1])
            fin(blocks[-1])
            nc.sync.dma_start(out=c_out[:, :], in_=cn[:])

        def drain_o(blocks):
            for blk in blocks:
                add_bias(3, blk)
                nc.scalar.activation(out=zt[blk][:], in_=zt[blk][:], func=ACT.Sigmoid)
            for blk in blocks:
                nc.vector.tensor_tensor(out=hn[:, cols(blk)], in0=zt[blk][:], in1=tcn[:, cols(blk)], op=ALU.mult)
            lo = blocks[0][0]
            hi = blocks[-1][0] + blocks[-1][1]
            nc.sync.dma_start(out=h_out[:, lo:hi], in_=hn[:, lo:hi])

        drains = [drain_i, drain_g, drain_f, drain_o]
        loaded = NB
        for u in range(len(units)):
            s, gi, passes = units[u]
            wt = wtiles[u]
            lo = GROUPS[s][gi][0][0]
            for j, cp in enumerate(passes):
                if cp < 2:
                    idx = 4 + s // 2
                    k = 8 * (s % 2) + 4 * cp
                else:
                    idx = s
                    k = 4 * (cp - 2)
                for blk in GROUPS[s][gi]:
                    if cp == 0:
                        banks[(s, blk)] = psum.tile([P, blk[1]], F32, name="acc%d_%d" % (s, blk[0]), tag="bk%d" % blk[2])
                    nc.tensor.matmul_mx(
                        out=banks[(s, blk)][:],
                        lhsT=a_codes[:, P * cp : P * (cp + 1)].bitcast(FP8X4),
                        lhsT_scale=a_scl[:, P * cp : P * (cp + 1)],
                        rhs=wt[:, j, blk[0] - lo : blk[0] - lo + blk[1]].bitcast(FP8X4),
                        rhs_scale=planes[k:P, idx, cols(blk)],
                        start=(cp == 0),
                        stop=(cp == PASSES - 1),
                    )
            want = len(units) if u + NB >= 3 * PASSES + PASSES - 1 else u + NB + 1
            while loaded < want:
                load(loaded)
                loaded += 1
            if u == 3:
                for m in range(16):
                    bias_block(m)
            if passes[-1] == PASSES - 1:
                drains[s](GROUPS[s][gi])
